import numpy as np
import ml_dtypes

BF16 = ml_dtypes.bfloat16


def bf(x):
    return np.asarray(x, np.float32).astype(BF16)


def f32(x):
    return np.asarray(x, np.float32)


def f64(x):
    return np.asarray(x).astype(np.float64)


def striped(idx):
    return np.tile(idx.reshape(-1, 16).T, (8, 1))


C, S, N, D, E, B = 512, 1024, 512, 256, 4, 128
NOISE_EPS = 0.01
KAPPA = np.log(2.0) + NOISE_EPS
MARGIN = 0.002
TINY = 1e-8


def soft(z):
    p = np.exp(KAPPA * z)
    return p / p.sum(axis=0, keepdims=True)


def draw_noise():
    z = f32(np.random.standard_normal((E, B)))
    while True:
        bad = (np.abs(soft(f64(z)) - 1.0 / E) < MARGIN).any(axis=0)
        if not bad.any():
            return z.reshape(1, N)
        z[:, bad] = f32(np.random.standard_normal((E, int(bad.sum()))))


def setup_inputs():
    return {"base": f32(np.random.standard_normal((C, S))), "x": bf(np.random.standard_normal((D, B))), "w1": bf(np.random.standard_normal((E, D, C)) / np.sqrt(D)), "b1": f32(0.1 * np.random.standard_normal((C, E))), "noise": draw_noise(), "offs": striped(np.random.permutation(S)[:N])}


def reference(base, x, w1, b1, noise, offs):
    idx = offs[:16].T.reshape(-1)
    p = soft(f64(noise).reshape(E, B))
    kept = np.where(p >= p.mean(axis=0, keepdims=True) - TINY, p, 0.0)
    gates = kept / kept.sum(axis=0, keepdims=True)
    h = np.tanh(np.einsum("edc,db->ceb", f64(w1), f64(x)) + f64(b1)[:, :, None])
    out = f64(base).copy()
    out[:, idx] = (h * gates[None]).reshape(C, N)
    return out

@@ -1,0 +1,99 @@
+import math
+
+import concourse.mybir as mybir
+
+F32 = mybir.dt.float32
+BF16 = mybir.dt.bfloat16
+U16 = mybir.dt.uint16
+ALU = mybir.AluOpType
+ACT = mybir.ActivationFunctionType
+AXIS = mybir.AxisListType
+
+P = 128
+C, S, N, D, E, B = 512, 1024, 512, 256, 4, 128
+C_BLOCKS = C // P
+D_BLOCKS = D // P
+KAPPA = math.log(2.0) + 0.01
+CUT = 1.0 / E - 1e-8
+
+FLOPS = 2 * E * D * C * B
+
+
+def tile_mblfe_kernel(tc, base, x, w1, b1, noise, offs, out):
+    nc = tc.nc
+    with (
+        tc.tile_pool(name="held", bufs=1) as held,
+        tc.tile_pool(name="hidden", bufs=2) as hidden,
+        tc.psum_pool(name="psum", bufs=2) as psum,
+    ):
+        offsets = held.tile([P, N // 16], U16, name="offsets")
+        nc.sync.dma_start(offsets[:], offs)
+
+        noise_all = held.tile([P, N], F32, name="noise_all")
+        nc.sync.dma_start(noise_all[:], noise.broadcast_to([P, N]))
+
+        x_sb = held.tile([P, D_BLOCKS, B], BF16, name="x_sb")
+        nc.sync.dma_start(x_sb[:], x.rearrange("(k p) b -> p k b", p=P))
+
+        bias_sb = held.tile([P, C_BLOCKS, E], F32, name="bias_sb")
+        nc.sync.dma_start(bias_sb[:], b1.rearrange("(cb p) e -> p cb e", p=P))
+
+        w_sb = held.tile([P, E, D_BLOCKS, C], BF16, name="w_sb")
+        for e in range(E):
+            nc.scalar.dma_start(w_sb[:, e, :, :], w1[e].rearrange("(k p) c -> p k c", p=P))
+
+        windows = []
+        for cb in range(C_BLOCKS):
+            window = held.tile([P, S], F32, name=f"window{cb}")
+            nc.sync.dma_start(window[:], base[cb * P : (cb + 1) * P, :])
+            windows.append(window)
+
+        def by_token(tile_ap):
+            return tile_ap.rearrange("p (e b) -> p b e", e=E)
+
+        def by_expert(tile_ap):
+            return tile_ap.rearrange("p (e b) -> p e b", e=E)
+
+        def over_experts(per_token):
+            return per_token.unsqueeze(1).to_broadcast([P, E, B])
+
+        top = held.tile([P, B], F32, name="top")
+        nc.vector.tensor_reduce(top[:], by_token(noise_all[:]), AXIS.X, ALU.max)
+        shifted = held.tile([P, N], F32, name="shifted")
+        nc.vector.tensor_tensor(by_expert(shifted[:]), by_expert(noise_all[:]), over_experts(top[:]), ALU.subtract)
+        ex = held.tile([P, N], F32, name="ex")
+        nc.scalar.activation(ex[:], shifted[:], ACT.Exp, scale=KAPPA)
+        cut = held.tile([P, B], F32, name="cut")
+        nc.vector.tensor_reduce(cut[:], by_token(ex[:]), AXIS.X, ALU.add)
+        nc.vector.tensor_scalar(cut[:], cut[:], CUT, None, ALU.mult)
+        kept = held.tile([P, N], F32, name="kept")
+        nc.vector.tensor_tensor(by_expert(kept[:]), by_expert(ex[:]), over_experts(cut[:]), ALU.is_ge)
+        nc.vector.tensor_tensor(kept[:], kept[:], ex[:], ALU.mult)
+        norm = held.tile([P, B], F32, name="norm")
+        nc.vector.tensor_reduce(norm[:], by_token(kept[:]), AXIS.X, ALU.add)
+        nc.vector.reciprocal(norm[:], norm[:])
+        gates = held.tile([P, N], F32, name="gates")
+        nc.vector.tensor_tensor(by_expert(gates[:]), by_expert(kept[:]), over_experts(norm[:]), ALU.mult)
+
+        for cb in range(C_BLOCKS):
+            channels = slice(cb * P, (cb + 1) * P)
+            product = psum.tile([P, N], F32, name="product")
+            for e in range(E):
+                for k in range(D_BLOCKS):
+                    nc.tensor.matmul(
+                        product[:, e * B : (e + 1) * B],
+                        w_sb[:, e, k, channels],
+                        x_sb[:, k, :],
+                        start=(k == 0),
+                        stop=(k == D_BLOCKS - 1),
+                    )
+            h = hidden.tile([P, N], F32, name="h")
+            for e in range(E):
+                nc.scalar.activation(
+                    h[:, e * B : (e + 1) * B],
+                    product[:, e * B : (e + 1) * B],
+                    ACT.Tanh,
+                    bias=bias_sb[:, cb, e : e + 1],
+                )
+            nc.vector.tensor_tensor(windows[cb][:].indirect(offsets[:]), h[:], gates[:], ALU.mult)
+            nc.sync.dma_start(out[channels, :], windows[cb][:])

@@ -1,6 +1,7 @@
 import math
 
 import concourse.mybir as mybir
+from concourse.masks import make_identity
 
 F32 = mybir.dt.float32
 BF16 = mybir.dt.bfloat16
@@ -26,54 +27,55 @@ def tile_mblfe_kernel(tc, base, x, w1, b1, noise, offs, out):
         tc.tile_pool(name="hidden", bufs=2) as hidden,
         tc.psum_pool(name="psum", bufs=2) as psum,
     ):
+        identity = held.tile([P, P], F32, name="identity")
+        make_identity(nc, identity[:])
+        ones = held.tile([P, P], F32, name="ones")
+        nc.gpsimd.memset(ones[:], 1.0)
+
         offsets = held.tile([P, N // 16], U16, name="offsets")
         nc.sync.dma_start(offsets[:], offs)
 
-        noise_all = held.tile([P, N], F32, name="noise_all")
-        nc.sync.dma_start(noise_all[:], noise.broadcast_to([P, N]))
+        score = held.tile([P, E], F32, name="score")
+        with nc.allow_non_contiguous_dma(reason="512 scores, one token to a partition"):
+            nc.scalar.dma_start(score[:], noise.rearrange("o (e b) -> (o b) e", e=E))
 
         x_sb = held.tile([P, D_BLOCKS, B], BF16, name="x_sb")
         nc.sync.dma_start(x_sb[:], x.rearrange("(k p) b -> p k b", p=P))
 
         bias_sb = held.tile([P, C_BLOCKS, E], F32, name="bias_sb")
-        nc.sync.dma_start(bias_sb[:], b1.rearrange("(cb p) e -> p cb e", p=P))
+        nc.scalar.dma_start(bias_sb[:], b1.rearrange("(cb p) e -> p cb e", p=P))
 
+        queues = (nc.sync, nc.scalar)
         w_sb = held.tile([P, E, D_BLOCKS, C], BF16, name="w_sb")
         for e in range(E):
-            nc.scalar.dma_start(w_sb[:, e, :, :], w1[e].rearrange("(k p) c -> p k c", p=P))
+            queues[e % 2].dma_start(w_sb[:, e, :, :], w1[e].rearrange("(k p) c -> p k c", p=P))
 
         windows = []
         for cb in range(C_BLOCKS):
             window = held.tile([P, S], F32, name=f"window{cb}")
-            nc.sync.dma_start(window[:], base[cb * P : (cb + 1) * P, :])
+            queues[cb % 2].dma_start(window[:], base[cb * P : (cb + 1) * P, :])
             windows.append(window)
 
-        def by_token(tile_ap):
-            return tile_ap.rearrange("p (e b) -> p b e", e=E)
-
-        def by_expert(tile_ap):
-            return tile_ap.rearrange("p (e b) -> p e b", e=E)
-
-        def over_experts(per_token):
-            return per_token.unsqueeze(1).to_broadcast([P, E, B])
-
-        top = held.tile([P, B], F32, name="top")
-        nc.vector.tensor_reduce(top[:], by_token(noise_all[:]), AXIS.X, ALU.max)
-        shifted = held.tile([P, N], F32, name="shifted")
-        nc.vector.tensor_tensor(by_expert(shifted[:]), by_expert(noise_all[:]), over_experts(top[:]), ALU.subtract)
-        ex = held.tile([P, N], F32, name="ex")
-        nc.scalar.activation(ex[:], shifted[:], ACT.Exp, scale=KAPPA)
-        cut = held.tile([P, B], F32, name="cut")
-        nc.vector.tensor_reduce(cut[:], by_token(ex[:]), AXIS.X, ALU.add)
-        nc.vector.tensor_scalar(cut[:], cut[:], CUT, None, ALU.mult)
-        kept = held.tile([P, N], F32, name="kept")
-        nc.vector.tensor_tensor(by_expert(kept[:]), by_expert(ex[:]), over_experts(cut[:]), ALU.is_ge)
-        nc.vector.tensor_tensor(kept[:], kept[:], ex[:], ALU.mult)
-        norm = held.tile([P, B], F32, name="norm")
-        nc.vector.tensor_reduce(norm[:], by_token(kept[:]), AXIS.X, ALU.add)
+        top = held.tile([P, 1], F32, name="top")
+        nc.vector.tensor_reduce(top[:], score[:], AXIS.X, ALU.max)
+        shifted = held.tile([P, E], F32, name="shifted")
+        nc.vector.tensor_scalar(shifted[:], score[:], top[:], None, ALU.subtract)
+        ex = held.tile([P, E], F32, name="ex")
+        total = held.tile([P, 1], F32, name="total")
+        nc.scalar.activation(ex[:], shifted[:], ACT.Exp, scale=KAPPA, accum_out=total[:])
+        cut = held.tile([P, 1], F32, name="cut")
+        nc.vector.tensor_scalar(cut[:], total[:], CUT, None, ALU.mult)
+        kept = held.tile([P, E], F32, name="kept")
+        norm = held.tile([P, 1], F32, name="norm")
+        nc.vector.scalar_tensor_tensor(kept[:], ex[:], cut[:], ex[:], ALU.is_ge, ALU.mult, accum_out=norm[:])
         nc.vector.reciprocal(norm[:], norm[:])
+        diagonal = held.tile([P, E, B], F32, name="diagonal")
+        for e in range(E):
+            nc.vector.tensor_scalar(diagonal[:, e, :], identity[:], kept[:, e : e + 1], norm[:], ALU.mult, ALU.mult)
+        spread = psum.tile([P, N], F32, name="spread")
+        nc.tensor.matmul(spread[:], ones[:], diagonal[:].rearrange("p e b -> p (e b)"), start=True, stop=True)
         gates = held.tile([P, N], F32, name="gates")
-        nc.vector.tensor_tensor(by_expert(gates[:]), by_expert(kept[:]), over_experts(norm[:]), ALU.mult)
+        nc.vector.tensor_copy(gates[:], spread[:])
 
         for cb in range(C_BLOCKS):
             channels = slice(cb * P, (cb + 1) * P)

@@ -16,6 +16,7 @@ C_BLOCKS = C // P
 D_BLOCKS = D // P
 KAPPA = math.log(2.0) + 0.01
 CUT = 1.0 / E - 1e-8
+WARM_MATMULS = 6
 
 FLOPS = 2 * E * D * C * B
 
@@ -25,36 +26,43 @@ def tile_mblfe_kernel(tc, base, x, w1, b1, noise, offs, out):
     with (
         tc.tile_pool(name="held", bufs=1) as held,
         tc.tile_pool(name="hidden", bufs=2) as hidden,
+        tc.psum_pool(name="once", bufs=1) as once,
         tc.psum_pool(name="psum", bufs=2) as psum,
     ):
-        identity = held.tile([P, P], F32, name="identity")
-        make_identity(nc, identity[:])
-        ones = held.tile([P, P], F32, name="ones")
-        nc.gpsimd.memset(ones[:], 1.0)
-
-        offsets = held.tile([P, N // 16], U16, name="offsets")
-        nc.sync.dma_start(offsets[:], offs)
-
         score = held.tile([P, E], F32, name="score")
         with nc.allow_non_contiguous_dma(reason="512 scores, one token to a partition"):
             nc.scalar.dma_start(score[:], noise.rearrange("o (e b) -> (o b) e", e=E))
 
-        x_sb = held.tile([P, D_BLOCKS, B], BF16, name="x_sb")
-        nc.sync.dma_start(x_sb[:], x.rearrange("(k p) b -> p k b", p=P))
-
         bias_sb = held.tile([P, C_BLOCKS, E], F32, name="bias_sb")
         nc.scalar.dma_start(bias_sb[:], b1.rearrange("(cb p) e -> p cb e", p=P))
 
-        queues = (nc.sync, nc.scalar)
+        offsets = held.tile([P, N // 16], U16, name="offsets")
+        nc.sync.dma_start(offsets[:], offs)
+
+        x_sb = held.tile([P, D_BLOCKS, B], BF16, name="x_sb")
+        nc.sync.dma_start(x_sb[:], x.rearrange("(k p) b -> p k b", p=P))
+
         w_sb = held.tile([P, E, D_BLOCKS, C], BF16, name="w_sb")
         for e in range(E):
-            queues[e % 2].dma_start(w_sb[:, e, :, :], w1[e].rearrange("(k p) c -> p k c", p=P))
+            nc.sync.dma_start(w_sb[:, e, :, :], w1[e].rearrange("(k p) c -> p k c", p=P))
 
         windows = []
         for cb in range(C_BLOCKS):
             window = held.tile([P, S], F32, name=f"window{cb}")
-            queues[cb % 2].dma_start(window[:], base[cb * P : (cb + 1) * P, :])
+            nc.sync.dma_start(window[:], base[cb * P : (cb + 1) * P, :])
             windows.append(window)
+
+        identity = held.tile([P, P], F32, name="identity")
+        make_identity(nc, identity[:])
+        ones = held.tile([P, P], F32, name="ones")
+        nc.gpsimd.memset(ones[:], 1.0)
+        woken = held.tile([P, 1], F32, name="woken")
+        nc.scalar.activation(woken[:], ones[:, 0:1], ACT.Exp)
+        zeros = held.tile([P, N], BF16, name="zeros")
+        nc.vector.memset(zeros[:], 0.0)
+        unused = once.tile([P, N], F32, name="unused")
+        for turn in range(WARM_MATMULS):
+            nc.tensor.matmul(unused[:], zeros[:, 0:P], zeros[:], start=True, stop=True)
 
         top = held.tile([P, 1], F32, name="top")
         nc.vector.tensor_reduce(top[:], score[:], AXIS.X, ALU.max)
@@ -72,7 +80,7 @@ def tile_mblfe_kernel(tc, base, x, w1, b1, noise, offs, out):
         diagonal = held.tile([P, E, B], F32, name="diagonal")
         for e in range(E):
             nc.vector.tensor_scalar(diagonal[:, e, :], identity[:], kept[:, e : e + 1], norm[:], ALU.mult, ALU.mult)
-        spread = psum.tile([P, N], F32, name="spread")
+        spread = once.tile([P, N], F32, name="spread")
         nc.tensor.matmul(spread[:], ones[:], diagonal[:].rearrange("p e b -> p (e b)"), start=True, stop=True)
         gates = held.tile([P, N], F32, name="gates")
         nc.vector.tensor_copy(gates[:], spread[:])

@@ -80,14 +80,14 @@ def tile_mblfe_kernel(tc, base, x, w1, b1, noise, offs, out):
         diagonal = held.tile([P, E, B], F32, name="diagonal")
         for e in range(E):
             nc.vector.tensor_scalar(diagonal[:, e, :], identity[:], kept[:, e : e + 1], norm[:], ALU.mult, ALU.mult)
-        spread = once.tile([P, N], F32, name="spread")
+        spread = psum.tile([P, N], F32, name="spread", tag="bank")
         nc.tensor.matmul(spread[:], ones[:], diagonal[:].rearrange("p e b -> p (e b)"), start=True, stop=True)
         gates = held.tile([P, N], F32, name="gates")
         nc.vector.tensor_copy(gates[:], spread[:])
 
         for cb in range(C_BLOCKS):
             channels = slice(cb * P, (cb + 1) * P)
-            product = psum.tile([P, N], F32, name="product")
+            product = psum.tile([P, N], F32, name="product", tag="bank")
             for e in range(E):
                 for k in range(D_BLOCKS):
                     nc.tensor.matmul(

@@ -31,10 +31,7 @@ def tile_mblfe_kernel(tc, base, x, w1, b1, noise, offs, out):
     ):
         score = held.tile([P, E], F32, name="score")
         with nc.allow_non_contiguous_dma(reason="512 scores, one token to a partition"):
-            nc.scalar.dma_start(score[:], noise.rearrange("o (e b) -> (o b) e", e=E))
-
-        bias_sb = held.tile([P, C_BLOCKS, E], F32, name="bias_sb")
-        nc.scalar.dma_start(bias_sb[:], b1.rearrange("(cb p) e -> p cb e", p=P))
+            nc.sync.dma_start(score[:], noise.rearrange("o (e b) -> (o b) e", e=E))
 
         offsets = held.tile([P, N // 16], U16, name="offsets")
         nc.sync.dma_start(offsets[:], offs)
@@ -42,14 +39,18 @@ def tile_mblfe_kernel(tc, base, x, w1, b1, noise, offs, out):
         x_sb = held.tile([P, D_BLOCKS, B], BF16, name="x_sb")
         nc.sync.dma_start(x_sb[:], x.rearrange("(k p) b -> p k b", p=P))
 
-        w_sb = held.tile([P, E, D_BLOCKS, C], BF16, name="w_sb")
-        for e in range(E):
-            nc.sync.dma_start(w_sb[:, e, :, :], w1[e].rearrange("(k p) c -> p k c", p=P))
+        bias_sb = held.tile([P, C_BLOCKS, E], F32, name="bias_sb")
+        nc.sync.dma_start(bias_sb[:], b1.rearrange("(cb p) e -> p cb e", p=P))
 
+        weights = []
         windows = []
         for cb in range(C_BLOCKS):
+            channels = slice(cb * P, (cb + 1) * P)
+            w_sb = held.tile([P, E * D_BLOCKS, P], BF16, name=f"w_sb{cb}")
+            nc.sync.dma_start(w_sb[:], w1[:, :, channels].rearrange("e (k p) c -> p (e k) c", p=P))
+            weights.append(w_sb)
             window = held.tile([P, S], F32, name=f"window{cb}")
-            nc.sync.dma_start(window[:], base[cb * P : (cb + 1) * P, :])
+            nc.sync.dma_start(window[:], base[channels, :])
             windows.append(window)
 
         identity = held.tile([P, P], F32, name="identity")
@@ -92,7 +93,7 @@ def tile_mblfe_kernel(tc, base, x, w1, b1, noise, offs, out):
                 for k in range(D_BLOCKS):
                     nc.tensor.matmul(
                         product[:, e * B : (e + 1) * B],
-                        w_sb[:, e, k, channels],
+                        weights[cb][:, e * D_BLOCKS + k, :],
                         x_sb[:, k, :],
                         start=(k == 0),
                         stop=(k == D_BLOCKS - 1),

@@ -16,7 +16,7 @@ C_BLOCKS = C // P
 D_BLOCKS = D // P
 KAPPA = math.log(2.0) + 0.01
 CUT = 1.0 / E - 1e-8
-WARM_MATMULS = 6
+WARM_MATMULS = 3
 
 FLOPS = 2 * E * D * C * B
 
@@ -33,32 +33,28 @@ def tile_mblfe_kernel(tc, base, x, w1, b1, noise, offs, out):
         with nc.allow_non_contiguous_dma(reason="512 scores, one token to a partition"):
             nc.sync.dma_start(score[:], noise.rearrange("o (e b) -> (o b) e", e=E))
 
-        offsets = held.tile([P, N // 16], U16, name="offsets")
-        nc.sync.dma_start(offsets[:], offs)
-
         x_sb = held.tile([P, D_BLOCKS, B], BF16, name="x_sb")
         nc.sync.dma_start(x_sb[:], x.rearrange("(k p) b -> p k b", p=P))
 
+        weights = [held.tile([P, E * D_BLOCKS, P], BF16, name=f"w_sb{cb}") for cb in range(C_BLOCKS)]
+        windows = [held.tile([P, S], F32, name=f"window{cb}") for cb in range(C_BLOCKS)]
         bias_sb = held.tile([P, C_BLOCKS, E], F32, name="bias_sb")
-        nc.sync.dma_start(bias_sb[:], b1.rearrange("(cb p) e -> p cb e", p=P))
+        offsets = held.tile([P, N // 16], U16, name="offsets")
 
-        weights = []
-        windows = []
         for cb in range(C_BLOCKS):
             channels = slice(cb * P, (cb + 1) * P)
-            w_sb = held.tile([P, E * D_BLOCKS, P], BF16, name=f"w_sb{cb}")
-            nc.sync.dma_start(w_sb[:], w1[:, :, channels].rearrange("e (k p) c -> p (e k) c", p=P))
-            weights.append(w_sb)
-            window = held.tile([P, S], F32, name=f"window{cb}")
-            nc.sync.dma_start(window[:], base[channels, :])
-            windows.append(window)
+            nc.sync.dma_start(weights[cb][:], w1[:, :, channels].rearrange("e (k p) c -> p (e k) c", p=P))
+            if cb == 0:
+                nc.sync.dma_start(bias_sb[:], b1.rearrange("(cb p) e -> p cb e", p=P))
+                nc.sync.dma_start(offsets[:], offs)
+            nc.sync.dma_start(windows[cb][:], base[channels, :])
 
         identity = held.tile([P, P], F32, name="identity")
         make_identity(nc, identity[:])
-        ones = held.tile([P, P], F32, name="ones")
+        ones = held.tile([P, 1], F32, name="ones")
         nc.gpsimd.memset(ones[:], 1.0)
         woken = held.tile([P, 1], F32, name="woken")
-        nc.scalar.activation(woken[:], ones[:, 0:1], ACT.Exp)
+        nc.scalar.activation(woken[:], ones[:], ACT.Exp)
         zeros = held.tile([P, N], BF16, name="zeros")
         nc.vector.memset(zeros[:], 0.0)
         unused = once.tile([P, N], F32, name="unused")
@@ -78,16 +74,16 @@ def tile_mblfe_kernel(tc, base, x, w1, b1, noise, offs, out):
         norm = held.tile([P, 1], F32, name="norm")
         nc.vector.scalar_tensor_tensor(kept[:], ex[:], cut[:], ex[:], ALU.is_ge, ALU.mult, accum_out=norm[:])
         nc.vector.reciprocal(norm[:], norm[:])
-        diagonal = held.tile([P, E, B], F32, name="diagonal")
-        for e in range(E):
-            nc.vector.tensor_scalar(diagonal[:, e, :], identity[:], kept[:, e : e + 1], norm[:], ALU.mult, ALU.mult)
+        gate = held.tile([P, E], F32, name="gate")
+        nc.vector.tensor_scalar(gate[:], kept[:], norm[:], None, ALU.mult)
+
         spread = psum.tile([P, N], F32, name="spread", tag="bank")
-        nc.tensor.matmul(spread[:], ones[:], diagonal[:].rearrange("p e b -> p (e b)"), start=True, stop=True)
+        for e in range(E):
+            nc.tensor.transpose(spread[:, e * B : (e + 1) * B], gate[:, e : e + 1].to_broadcast([P, P]), identity[:])
         gates = held.tile([P, N], F32, name="gates")
         nc.vector.tensor_copy(gates[:], spread[:])
 
-        for cb in range(C_BLOCKS):
-            channels = slice(cb * P, (cb + 1) * P)
+        def hidden_layer(cb):
             product = psum.tile([P, N], F32, name="product", tag="bank")
             for e in range(E):
                 for k in range(D_BLOCKS):
@@ -106,5 +102,12 @@ def tile_mblfe_kernel(tc, base, x, w1, b1, noise, offs, out):
                     ACT.Tanh,
                     bias=bias_sb[:, cb, e : e + 1],
                 )
+            return h
+
+        h_next = hidden_layer(0)
+        for cb in range(C_BLOCKS):
+            h = h_next
+            if cb + 1 < C_BLOCKS:
+                h_next = hidden_layer(cb + 1)
             nc.vector.tensor_tensor(windows[cb][:].indirect(offsets[:]), h[:], gates[:], ALU.mult)
-            nc.sync.dma_start(out[channels, :], windows[cb][:])
+            nc.sync.dma_start(out[cb * P : (cb + 1) * P, :], windows[cb][:])

@@ -16,7 +16,7 @@ C_BLOCKS = C // P
 D_BLOCKS = D // P
 KAPPA = math.log(2.0) + 0.01
 CUT = 1.0 / E - 1e-8
-WARM_MATMULS = 3
+WARM_MATMULS = 6
 
 FLOPS = 2 * E * D * C * B
 
@@ -49,14 +49,14 @@ def tile_mblfe_kernel(tc, base, x, w1, b1, noise, offs, out):
                 nc.sync.dma_start(offsets[:], offs)
             nc.sync.dma_start(windows[cb][:], base[channels, :])
 
-        identity = held.tile([P, P], F32, name="identity")
-        make_identity(nc, identity[:])
+        zeros = held.tile([P, N], BF16, name="zeros")
+        nc.gpsimd.memset(zeros[:], 0.0)
         ones = held.tile([P, 1], F32, name="ones")
         nc.gpsimd.memset(ones[:], 1.0)
+        identity = held.tile([P, P], F32, name="identity")
+        make_identity(nc, identity[:])
         woken = held.tile([P, 1], F32, name="woken")
         nc.scalar.activation(woken[:], ones[:], ACT.Exp)
-        zeros = held.tile([P, N], BF16, name="zeros")
-        nc.vector.memset(zeros[:], 0.0)
         unused = once.tile([P, N], F32, name="unused")
         for turn in range(WARM_MATMULS):
             nc.tensor.matmul(unused[:], zeros[:, 0:P], zeros[:], start=True, stop=True)

@@ -8,7 +8,6 @@ BF16 = mybir.dt.bfloat16
 U16 = mybir.dt.uint16
 ALU = mybir.AluOpType
 ACT = mybir.ActivationFunctionType
-AXIS = mybir.AxisListType
 
 P = 128
 C, S, N, D, E, B = 512, 1024, 512, 256, 4, 128
@@ -61,15 +60,16 @@ def tile_mblfe_kernel(tc, base, x, w1, b1, noise, offs, out):
         for turn in range(WARM_MATMULS):
             nc.tensor.matmul(unused[:], zeros[:, 0:P], zeros[:], start=True, stop=True)
 
-        top = held.tile([P, 1], F32, name="top")
-        nc.vector.tensor_reduce(top[:], score[:], AXIS.X, ALU.max)
-        shifted = held.tile([P, E], F32, name="shifted")
-        nc.vector.tensor_scalar(shifted[:], score[:], top[:], None, ALU.subtract)
+        negated = held.tile([P, E], F32, name="negated")
+        shift = held.tile([P, 1], F32, name="shift")
+        nc.vector.tensor_scalar(negated[:], score[:], -KAPPA, None, ALU.mult, ALU.min, accum_out=shift[:])
+        lowered = held.tile([P, E], F32, name="lowered")
+        nc.vector.tensor_scalar(lowered[:], score[:], math.log(CUT) / KAPPA, None, ALU.add)
         ex = held.tile([P, E], F32, name="ex")
-        total = held.tile([P, 1], F32, name="total")
-        nc.scalar.activation(ex[:], shifted[:], ACT.Exp, scale=KAPPA, accum_out=total[:])
+        nc.scalar.activation(ex[:], score[:], ACT.Exp, bias=shift[:], scale=KAPPA)
+        ex_cut = held.tile([P, E], F32, name="ex_cut")
         cut = held.tile([P, 1], F32, name="cut")
-        nc.vector.tensor_scalar(cut[:], total[:], CUT, None, ALU.mult)
+        nc.scalar.activation(ex_cut[:], lowered[:], ACT.Exp, bias=shift[:], scale=KAPPA, accum_out=cut[:])
         kept = held.tile([P, E], F32, name="kept")
         norm = held.tile([P, 1], F32, name="norm")
         nc.vector.scalar_tensor_tensor(kept[:], ex[:], cut[:], ex[:], ALU.is_ge, ALU.mult, accum_out=norm[:])

@@ -13,6 +13,7 @@ P = 128
 C, S, N, D, E, B = 512, 1024, 512, 256, 4, 128
 C_BLOCKS = C // P
 D_BLOCKS = D // P
+HALVES = 2
 KAPPA = math.log(2.0) + 0.01
 CUT = 1.0 / E - 1e-8
 WARM_MATMULS = 6
@@ -77,31 +78,39 @@ def tile_mblfe_kernel(tc, base, x, w1, b1, noise, offs, out):
         gate = held.tile([P, E], F32, name="gate")
         nc.vector.tensor_scalar(gate[:], kept[:], norm[:], None, ALU.mult)
 
-        spread = psum.tile([P, N], F32, name="spread", tag="bank")
-        for e in range(E):
-            nc.tensor.transpose(spread[:, e * B : (e + 1) * B], gate[:, e : e + 1].to_broadcast([P, P]), identity[:])
         gates = held.tile([P, N], F32, name="gates")
-        nc.vector.tensor_copy(gates[:], spread[:])
+        for half in range(HALVES):
+            spread = psum.tile([P, N // HALVES], F32, name="spread", tag="later")
+            for i in range(E // HALVES):
+                e = half * (E // HALVES) + i
+                nc.tensor.transpose(spread[:, i * B : (i + 1) * B], gate[:, e : e + 1].to_broadcast([P, P]), identity[:])
+            copied = gates[:, half * (N // HALVES) : (half + 1) * (N // HALVES)]
+            if half == 0:
+                nc.vector.tensor_copy(copied, spread[:])
+            else:
+                nc.scalar.copy(copied, spread[:])
 
         def hidden_layer(cb):
-            product = psum.tile([P, N], F32, name="product", tag="bank")
-            for e in range(E):
-                for k in range(D_BLOCKS):
-                    nc.tensor.matmul(
-                        product[:, e * B : (e + 1) * B],
-                        weights[cb][:, e * D_BLOCKS + k, :],
-                        x_sb[:, k, :],
-                        start=(k == 0),
-                        stop=(k == D_BLOCKS - 1),
-                    )
             h = hidden.tile([P, N], F32, name="h")
-            for e in range(E):
-                nc.scalar.activation(
-                    h[:, e * B : (e + 1) * B],
-                    product[:, e * B : (e + 1) * B],
-                    ACT.Tanh,
-                    bias=bias_sb[:, cb, e : e + 1],
-                )
+            for half in range(HALVES):
+                product = psum.tile([P, N // HALVES], F32, name="product", tag="first" if cb == 0 else "later")
+                experts = range(half * (E // HALVES), (half + 1) * (E // HALVES))
+                for i, e in enumerate(experts):
+                    for k in range(D_BLOCKS):
+                        nc.tensor.matmul(
+                            product[:, i * B : (i + 1) * B],
+                            weights[cb][:, e * D_BLOCKS + k, :],
+                            x_sb[:, k, :],
+                            start=(k == 0),
+                            stop=(k == D_BLOCKS - 1),
+                        )
+                for i, e in enumerate(experts):
+                    nc.scalar.activation(
+                        h[:, e * B : (e + 1) * B],
+                        product[:, i * B : (i + 1) * B],
+                        ACT.Tanh,
+                        bias=bias_sb[:, cb, e : e + 1],
+                    )
             return h
 
         h_next = hidden_layer(0)

@@ -27,7 +27,8 @@ def tile_mblfe_kernel(tc, base, x, w1, b1, noise, offs, out):
         tc.tile_pool(name="held", bufs=1) as held,
         tc.tile_pool(name="hidden", bufs=2) as hidden,
         tc.psum_pool(name="once", bufs=1) as once,
-        tc.psum_pool(name="psum", bufs=2) as psum,
+        tc.psum_pool(name="first", bufs=E) as first,
+        tc.psum_pool(name="later", bufs=HALVES) as later,
     ):
         score = held.tile([P, E], F32, name="score")
         with nc.allow_non_contiguous_dma(reason="512 scores, one token to a partition"):
@@ -80,7 +81,7 @@ def tile_mblfe_kernel(tc, base, x, w1, b1, noise, offs, out):
 
         gates = held.tile([P, N], F32, name="gates")
         for half in range(HALVES):
-            spread = psum.tile([P, N // HALVES], F32, name="spread", tag="later")
+            spread = later.tile([P, N // HALVES], F32, name="spread", tag="bank")
             for i in range(E // HALVES):
                 e = half * (E // HALVES) + i
                 nc.tensor.transpose(spread[:, i * B : (i + 1) * B], gate[:, e : e + 1].to_broadcast([P, P]), identity[:])
@@ -91,10 +92,11 @@ def tile_mblfe_kernel(tc, base, x, w1, b1, noise, offs, out):
                 nc.scalar.copy(copied, spread[:])
 
         def hidden_layer(cb):
+            banks, together = (first, 1) if cb == 0 else (later, E // HALVES)
             h = hidden.tile([P, N], F32, name="h")
-            for half in range(HALVES):
-                product = psum.tile([P, N // HALVES], F32, name="product", tag="first" if cb == 0 else "later")
-                experts = range(half * (E // HALVES), (half + 1) * (E // HALVES))
+            for lead in range(0, E, together):
+                product = banks.tile([P, together * B], F32, name="product", tag="bank")
+                experts = range(lead, lead + together)
                 for i, e in enumerate(experts):
                     for k in range(D_BLOCKS):
                         nc.tensor.matmul(

@@ -13,6 +13,7 @@ P = 128
 C, S, N, D, E, B = 512, 1024, 512, 256, 4, 128
 C_BLOCKS = C // P
 D_BLOCKS = D // P
+BLOCK = 8
 HALVES = 2
 KAPPA = math.log(2.0) + 0.01
 CUT = 1.0 / E - 1e-8
@@ -30,23 +31,24 @@ def tile_mblfe_kernel(tc, base, x, w1, b1, noise, offs, out):
         tc.psum_pool(name="first", bufs=E) as first,
         tc.psum_pool(name="later", bufs=HALVES) as later,
     ):
-        score = held.tile([P, E], F32, name="score")
+        score_blocks = held.tile([P, E, BLOCK], F32, name="score_blocks")
+        score = score_blocks[:, :, 0]
         with nc.allow_non_contiguous_dma(reason="512 scores, one token to a partition"):
-            nc.sync.dma_start(score[:], noise.rearrange("o (e b) -> (o b) e", e=E))
+            nc.sync.dma_start(score, noise.rearrange("o (e b) -> (o b) e", e=E))
 
         x_sb = held.tile([P, D_BLOCKS, B], BF16, name="x_sb")
         nc.sync.dma_start(x_sb[:], x.rearrange("(k p) b -> p k b", p=P))
 
         weights = [held.tile([P, E * D_BLOCKS, P], BF16, name=f"w_sb{cb}") for cb in range(C_BLOCKS)]
         windows = [held.tile([P, S], F32, name=f"window{cb}") for cb in range(C_BLOCKS)]
-        bias_sb = held.tile([P, C_BLOCKS, E], F32, name="bias_sb")
+        bias_sb = held.tile([P, C_BLOCKS, BLOCK], F32, name="bias_sb")
         offsets = held.tile([P, N // 16], U16, name="offsets")
 
         for cb in range(C_BLOCKS):
             channels = slice(cb * P, (cb + 1) * P)
             nc.sync.dma_start(weights[cb][:], w1[:, :, channels].rearrange("e (k p) c -> p (e k) c", p=P))
             if cb == 0:
-                nc.sync.dma_start(bias_sb[:], b1.rearrange("(cb p) e -> p cb e", p=P))
+                nc.sync.dma_start(bias_sb[:, :, 0:E], b1.rearrange("(cb p) e -> p cb e", p=P))
                 nc.sync.dma_start(offsets[:], offs)
             nc.sync.dma_start(windows[cb][:], base[channels, :])
 
@@ -64,11 +66,11 @@ def tile_mblfe_kernel(tc, base, x, w1, b1, noise, offs, out):
 
         negated = held.tile([P, E], F32, name="negated")
         shift = held.tile([P, 1], F32, name="shift")
-        nc.vector.tensor_scalar(negated[:], score[:], -KAPPA, None, ALU.mult, ALU.min, accum_out=shift[:])
+        nc.vector.tensor_scalar(negated[:], score, -KAPPA, None, ALU.mult, ALU.min, accum_out=shift[:])
         lowered = held.tile([P, E], F32, name="lowered")
-        nc.vector.tensor_scalar(lowered[:], score[:], math.log(CUT) / KAPPA, None, ALU.add)
+        nc.vector.tensor_scalar(lowered[:], score, math.log(CUT) / KAPPA, None, ALU.add)
         ex = held.tile([P, E], F32, name="ex")
-        nc.scalar.activation(ex[:], score[:], ACT.Exp, bias=shift[:], scale=KAPPA)
+        nc.scalar.activation(ex[:], score, ACT.Exp, bias=shift[:], scale=KAPPA)
         ex_cut = held.tile([P, E], F32, name="ex_cut")
         cut = held.tile([P, 1], F32, name="cut")
         nc.scalar.activation(ex_cut[:], lowered[:], ACT.Exp, bias=shift[:], scale=KAPPA, accum_out=cut[:])

@@ -39,18 +39,27 @@ def tile_mblfe_kernel(tc, base, x, w1, b1, noise, offs, out):
         x_sb = held.tile([P, D_BLOCKS, B], BF16, name="x_sb")
         nc.sync.dma_start(x_sb[:], x.rearrange("(k p) b -> p k b", p=P))
 
-        weights = [held.tile([P, E * D_BLOCKS, P], BF16, name=f"w_sb{cb}") for cb in range(C_BLOCKS)]
+        single = [held.tile([P, E * D_BLOCKS, P], BF16, name=f"w_sb{cb}") for cb in range(2)]
+        shared = held.tile([P, E * D_BLOCKS, 2 * P], BF16, name="w_sb23")
+        weights = [single[0][:], single[1][:], shared[:, :, 0:P], shared[:, :, P : 2 * P]]
         windows = [held.tile([P, S], F32, name=f"window{cb}") for cb in range(C_BLOCKS)]
-        bias_sb = held.tile([P, C_BLOCKS, BLOCK], F32, name="bias_sb")
+        first_bias = held.tile([P, 1, BLOCK], F32, name="first_bias")
+        later_bias = held.tile([P, C_BLOCKS - 1, BLOCK], F32, name="later_bias")
+        bias_sb = [first_bias[:, 0, :]] + [later_bias[:, cb - 1, :] for cb in range(1, C_BLOCKS)]
         offsets = held.tile([P, N // 16], U16, name="offsets")
 
         for cb in range(C_BLOCKS):
             channels = slice(cb * P, (cb + 1) * P)
-            nc.sync.dma_start(weights[cb][:], w1[:, :, channels].rearrange("e (k p) c -> p (e k) c", p=P))
+            if cb < 2:
+                nc.sync.dma_start(weights[cb], w1[:, :, channels].rearrange("e (k p) c -> p (e k) c", p=P))
+            elif cb == 2:
+                nc.sync.dma_start(shared[:], w1[:, :, 2 * P : C].rearrange("e (k p) c -> p (e k) c", p=P))
             if cb == 0:
-                nc.sync.dma_start(bias_sb[:, :, 0:E], b1.rearrange("(cb p) e -> p cb e", p=P))
+                nc.sync.dma_start(first_bias[:, 0, 0:E], b1[channels, :])
                 nc.sync.dma_start(offsets[:], offs)
             nc.sync.dma_start(windows[cb][:], base[channels, :])
+            if cb == 0:
+                nc.sync.dma_start(later_bias[:, :, 0:E], b1[P:C, :].rearrange("(cb p) e -> p cb e", p=P))
 
         zeros = held.tile([P, N], BF16, name="zeros")
         nc.gpsimd.memset(zeros[:], 0.0)
@@ -113,7 +122,7 @@ def tile_mblfe_kernel(tc, base, x, w1, b1, noise, offs, out):
                         h[:, e * B : (e + 1) * B],
                         product[:, i * B : (i + 1) * B],
                         ACT.Tanh,
-                        bias=bias_sb[:, cb, e : e + 1],
+                        bias=bias_sb[cb][:, e : e + 1],
                     )
             return h
 

@@ -39,30 +39,37 @@ def tile_mblfe_kernel(tc, base, x, w1, b1, noise, offs, out):
         x_sb = held.tile([P, D_BLOCKS, B], BF16, name="x_sb")
         nc.sync.dma_start(x_sb[:], x.rearrange("(k p) b -> p k b", p=P))
 
-        single = [held.tile([P, E * D_BLOCKS, P], BF16, name=f"w_sb{cb}") for cb in range(2)]
+        halves = [held.tile([P, E // HALVES * D_BLOCKS, P], BF16, name=f"w_sb0{half}") for half in range(HALVES)]
+        second = held.tile([P, E * D_BLOCKS, P], BF16, name="w_sb1")
         shared = held.tile([P, E * D_BLOCKS, 2 * P], BF16, name="w_sb23")
-        weights = [single[0][:], single[1][:], shared[:, :, 0:P], shared[:, :, P : 2 * P]]
+
+        def weight(cb, e, k):
+            row = e * D_BLOCKS + k
+            if cb == 0:
+                return halves[e // HALVES][:, row % (E // HALVES * D_BLOCKS), :]
+            if cb == 1:
+                return second[:, row, :]
+            return shared[:, row, (cb - 2) * P : (cb - 1) * P]
+
         windows = [held.tile([P, S], F32, name=f"window{cb}") for cb in range(C_BLOCKS)]
-        first_bias = held.tile([P, 1, BLOCK], F32, name="first_bias")
-        later_bias = held.tile([P, C_BLOCKS - 1, BLOCK], F32, name="later_bias")
-        bias_sb = [first_bias[:, 0, :]] + [later_bias[:, cb - 1, :] for cb in range(1, C_BLOCKS)]
+        bias_sb = held.tile([P, C_BLOCKS, BLOCK], F32, name="bias_sb")
         offsets = held.tile([P, N // 16], U16, name="offsets")
 
-        for cb in range(C_BLOCKS):
-            channels = slice(cb * P, (cb + 1) * P)
-            if cb < 2:
-                nc.sync.dma_start(weights[cb], w1[:, :, channels].rearrange("e (k p) c -> p (e k) c", p=P))
-            elif cb == 2:
-                nc.sync.dma_start(shared[:], w1[:, :, 2 * P : C].rearrange("e (k p) c -> p (e k) c", p=P))
-            if cb == 0:
-                nc.sync.dma_start(first_bias[:, 0, 0:E], b1[channels, :])
-                nc.sync.dma_start(offsets[:], offs)
-            nc.sync.dma_start(windows[cb][:], base[channels, :])
-            if cb == 0:
-                nc.sync.dma_start(later_bias[:, :, 0:E], b1[P:C, :].rearrange("(cb p) e -> p cb e", p=P))
+        for half in range(HALVES):
+            experts = slice(half * (E // HALVES), (half + 1) * (E // HALVES))
+            nc.sync.dma_start(halves[half][:], w1[experts, :, 0:P].rearrange("e (k p) c -> p (e k) c", p=P))
+            if half == 0:
+                nc.sync.dma_start(bias_sb[:, :, 0:E], b1.rearrange("(cb p) e -> p cb e", p=P))
+        nc.sync.dma_start(offsets[:], offs)
+        nc.sync.dma_start(windows[0][:], base[0:P, :])
+        nc.sync.dma_start(second[:], w1[:, :, P : 2 * P].rearrange("e (k p) c -> p (e k) c", p=P))
+        nc.sync.dma_start(windows[1][:], base[P : 2 * P, :])
+        nc.sync.dma_start(shared[:], w1[:, :, 2 * P : C].rearrange("e (k p) c -> p (e k) c", p=P))
+        for cb in range(2, C_BLOCKS):
+            nc.sync.dma_start(windows[cb][:], base[cb * P : (cb + 1) * P, :])
 
-        zeros = held.tile([P, N], BF16, name="zeros")
-        nc.gpsimd.memset(zeros[:], 0.0)
+        zero = held.tile([P, 1], BF16, name="zero")
+        nc.gpsimd.memset(zero[:], 0.0)
         ones = held.tile([P, 1], F32, name="ones")
         nc.gpsimd.memset(ones[:], 1.0)
         identity = held.tile([P, P], F32, name="identity")
@@ -71,7 +78,7 @@ def tile_mblfe_kernel(tc, base, x, w1, b1, noise, offs, out):
         nc.scalar.activation(woken[:], ones[:], ACT.Exp)
         unused = once.tile([P, N], F32, name="unused")
         for turn in range(WARM_MATMULS):
-            nc.tensor.matmul(unused[:], zeros[:, 0:P], zeros[:], start=True, stop=True)
+            nc.tensor.matmul(unused[:], zero[:].to_broadcast([P, P]), zero[:].to_broadcast([P, N]), start=True, stop=True)
 
         negated = held.tile([P, E], F32, name="negated")
         shift = held.tile([P, 1], F32, name="shift")
@@ -112,7 +119,7 @@ def tile_mblfe_kernel(tc, base, x, w1, b1, noise, offs, out):
                     for k in range(D_BLOCKS):
                         nc.tensor.matmul(
                             product[:, i * B : (i + 1) * B],
-                            weights[cb][:, e * D_BLOCKS + k, :],
+                            weight(cb, e, k),
                             x_sb[:, k, :],
                             start=(k == 0),
                             stop=(k == D_BLOCKS - 1),
@@ -122,7 +129,7 @@ def tile_mblfe_kernel(tc, base, x, w1, b1, noise, offs, out):
                         h[:, e * B : (e + 1) * B],
                         product[:, i * B : (i + 1) * B],
                         ACT.Tanh,
-                        bias=bias_sb[cb][:, e : e + 1],
+                        bias=bias_sb[:, cb, e : e + 1],
                     )
             return h
 

@@ -83,16 +83,16 @@ def tile_mblfe_kernel(tc, base, x, w1, b1, noise, offs, out):
         negated = held.tile([P, E], F32, name="negated")
         shift = held.tile([P, 1], F32, name="shift")
         nc.vector.tensor_scalar(negated[:], score, -KAPPA, None, ALU.mult, ALU.min, accum_out=shift[:])
-        lowered = held.tile([P, E], F32, name="lowered")
-        nc.vector.tensor_scalar(lowered[:], score, math.log(CUT) / KAPPA, None, ALU.add)
+        raised = held.tile([P, E], F32, name="raised")
+        nc.vector.tensor_scalar(raised[:], score, -math.log(CUT) / KAPPA, None, ALU.add)
         ex = held.tile([P, E], F32, name="ex")
-        nc.scalar.activation(ex[:], score, ACT.Exp, bias=shift[:], scale=KAPPA)
-        ex_cut = held.tile([P, E], F32, name="ex_cut")
-        cut = held.tile([P, 1], F32, name="cut")
-        nc.scalar.activation(ex_cut[:], lowered[:], ACT.Exp, bias=shift[:], scale=KAPPA, accum_out=cut[:])
+        total = held.tile([P, 1], F32, name="total")
+        nc.scalar.activation(ex[:], score, ACT.Exp, bias=shift[:], scale=KAPPA, accum_out=total[:])
+        ex_raised = held.tile([P, E], F32, name="ex_raised")
+        nc.scalar.activation(ex_raised[:], raised[:], ACT.Exp, bias=shift[:], scale=KAPPA)
         kept = held.tile([P, E], F32, name="kept")
         norm = held.tile([P, 1], F32, name="norm")
-        nc.vector.scalar_tensor_tensor(kept[:], ex[:], cut[:], ex[:], ALU.is_ge, ALU.mult, accum_out=norm[:])
+        nc.vector.scalar_tensor_tensor(kept[:], ex_raised[:], total[:], ex[:], ALU.is_ge, ALU.mult, accum_out=norm[:])
         nc.vector.reciprocal(norm[:], norm[:])
         gate = held.tile([P, E], F32, name="gate")
         nc.vector.tensor_scalar(gate[:], kept[:], norm[:], None, ALU.mult)

import math

import concourse.mybir as mybir
from concourse.masks import make_identity

F32 = mybir.dt.float32
BF16 = mybir.dt.bfloat16
U16 = mybir.dt.uint16
ALU = mybir.AluOpType
ACT = mybir.ActivationFunctionType

P = 128
C, S, N, D, E, B = 512, 1024, 512, 256, 4, 128
C_BLOCKS = C // P
D_BLOCKS = D // P
BLOCK = 8
HALVES = 2
KAPPA = math.log(2.0) + 0.01
CUT = 1.0 / E - 1e-8
WARM_MATMULS = 6

FLOPS = 2 * E * D * C * B


def tile_mblfe_kernel(tc, base, x, w1, b1, noise, offs, out):
    nc = tc.nc
    with (
        tc.tile_pool(name="held", bufs=1) as held,
        tc.tile_pool(name="hidden", bufs=2) as hidden,
        tc.psum_pool(name="once", bufs=1) as once,
        tc.psum_pool(name="first", bufs=E) as first,
        tc.psum_pool(name="later", bufs=HALVES) as later,
    ):
        score_blocks = held.tile([P, E, BLOCK], F32, name="score_blocks")
        score = score_blocks[:, :, 0]
        with nc.allow_non_contiguous_dma(reason="512 scores, one token to a partition"):
            nc.sync.dma_start(score, noise.rearrange("o (e b) -> (o b) e", e=E))

        x_sb = held.tile([P, D_BLOCKS, B], BF16, name="x_sb")
        nc.sync.dma_start(x_sb[:], x.rearrange("(k p) b -> p k b", p=P))

        halves = [held.tile([P, E // HALVES * D_BLOCKS, P], BF16, name=f"w_sb0{half}") for half in range(HALVES)]
        second = held.tile([P, E * D_BLOCKS, P], BF16, name="w_sb1")
        shared = held.tile([P, E * D_BLOCKS, 2 * P], BF16, name="w_sb23")

        def weight(cb, e, k):
            row = e * D_BLOCKS + k
            if cb == 0:
                return halves[e // HALVES][:, row % (E // HALVES * D_BLOCKS), :]
            if cb == 1:
                return second[:, row, :]
            return shared[:, row, (cb - 2) * P : (cb - 1) * P]

        windows = [held.tile([P, S], F32, name=f"window{cb}") for cb in range(C_BLOCKS)]
        bias_sb = held.tile([P, C_BLOCKS, BLOCK], F32, name="bias_sb")
        offsets = held.tile([P, N // 16], U16, name="offsets")

        for half in range(HALVES):
            experts = slice(half * (E // HALVES), (half + 1) * (E // HALVES))
            nc.sync.dma_start(halves[half][:], w1[experts, :, 0:P].rearrange("e (k p) c -> p (e k) c", p=P))
            if half == 0:
                nc.sync.dma_start(bias_sb[:, :, 0:E], b1.rearrange("(cb p) e -> p cb e", p=P))
        nc.sync.dma_start(offsets[:], offs)
        nc.sync.dma_start(windows[0][:], base[0:P, :])
        nc.sync.dma_start(second[:], w1[:, :, P : 2 * P].rearrange("e (k p) c -> p (e k) c", p=P))
        nc.sync.dma_start(windows[1][:], base[P : 2 * P, :])
        nc.sync.dma_start(shared[:], w1[:, :, 2 * P : C].rearrange("e (k p) c -> p (e k) c", p=P))
        for cb in range(2, C_BLOCKS):
            nc.sync.dma_start(windows[cb][:], base[cb * P : (cb + 1) * P, :])

        zero = held.tile([P, 1], BF16, name="zero")
        nc.gpsimd.memset(zero[:], 0.0)
        ones = held.tile([P, 1], F32, name="ones")
        nc.gpsimd.memset(ones[:], 1.0)
        identity = held.tile([P, P], F32, name="identity")
        make_identity(nc, identity[:])
        woken = held.tile([P, 1], F32, name="woken")
        nc.scalar.activation(woken[:], ones[:], ACT.Exp)
        unused = once.tile([P, N], F32, name="unused")
        for turn in range(WARM_MATMULS):
            nc.tensor.matmul(unused[:], zero[:].to_broadcast([P, P]), zero[:].to_broadcast([P, N]), start=True, stop=True)

        negated = held.tile([P, E], F32, name="negated")
        shift = held.tile([P, 1], F32, name="shift")
        nc.vector.tensor_scalar(negated[:], score, -KAPPA, None, ALU.mult, ALU.min, accum_out=shift[:])
        raised = held.tile([P, E], F32, name="raised")
        nc.vector.tensor_scalar(raised[:], score, -math.log(CUT) / KAPPA, None, ALU.add)
        ex = held.tile([P, E], F32, name="ex")
        total = held.tile([P, 1], F32, name="total")
        nc.scalar.activation(ex[:], score, ACT.Exp, bias=shift[:], scale=KAPPA, accum_out=total[:])
        ex_raised = held.tile([P, E], F32, name="ex_raised")
        nc.scalar.activation(ex_raised[:], raised[:], ACT.Exp, bias=shift[:], scale=KAPPA)
        kept = held.tile([P, E], F32, name="kept")
        norm = held.tile([P, 1], F32, name="norm")
        nc.vector.scalar_tensor_tensor(kept[:], ex_raised[:], total[:], ex[:], ALU.is_ge, ALU.mult, accum_out=norm[:])
        nc.vector.reciprocal(norm[:], norm[:])
        gate = held.tile([P, E], F32, name="gate")
        nc.vector.tensor_scalar(gate[:], kept[:], norm[:], None, ALU.mult)

        gates = held.tile([P, N], F32, name="gates")
        for half in range(HALVES):
            spread = later.tile([P, N // HALVES], F32, name="spread", tag="bank")
            for i in range(E // HALVES):
                e = half * (E // HALVES) + i
                nc.tensor.transpose(spread[:, i * B : (i + 1) * B], gate[:, e : e + 1].to_broadcast([P, P]), identity[:])
            copied = gates[:, half * (N // HALVES) : (half + 1) * (N // HALVES)]
            if half == 0:
                nc.vector.tensor_copy(copied, spread[:])
            else:
                nc.scalar.copy(copied, spread[:])

        def hidden_layer(cb):
            banks, together = (first, 1) if cb == 0 else (later, E // HALVES)
            h = hidden.tile([P, N], F32, name="h")
            for lead in range(0, E, together):
                product = banks.tile([P, together * B], F32, name="product", tag="bank")
                experts = range(lead, lead + together)
                for i, e in enumerate(experts):
                    for k in range(D_BLOCKS):
                        nc.tensor.matmul(
                            product[:, i * B : (i + 1) * B],
                            weight(cb, e, k),
                            x_sb[:, k, :],
                            start=(k == 0),
                            stop=(k == D_BLOCKS - 1),
                        )
                for i, e in enumerate(experts):
                    nc.scalar.activation(
                        h[:, e * B : (e + 1) * B],
                        product[:, i * B : (i + 1) * B],
                        ACT.Tanh,
                        bias=bias_sb[:, cb, e : e + 1],
                    )
            return h

        h_next = hidden_layer(0)
        for cb in range(C_BLOCKS):
            h = h_next
            if cb + 1 < C_BLOCKS:
                h_next = hidden_layer(cb + 1)
            nc.vector.tensor_tensor(windows[cb][:].indirect(offsets[:]), h[:], gates[:], ALU.mult)
            nc.sync.dma_start(out[cb * P : (cb + 1) * P, :], windows[cb][:])
